import numpy as np
import ml_dtypes


def mxq(x, axis, fmt="e4m3"):
    dtype, down = {"e4m3": (ml_dtypes.float8_e4m3fn, 7), "e5m2": (ml_dtypes.float8_e5m2, 14)}[fmt]
    v = np.moveaxis(np.asarray(x, np.float32).astype(ml_dtypes.bfloat16).astype(np.float64), axis, -1)
    blocks = v.reshape(v.shape[:-1] + (-1, 32))
    amax = np.abs(blocks).max(-1, keepdims=True)
    byte = np.maximum(np.where(amax > 0, np.frexp(amax)[1] - 1 + 127, 0) - down, 1)
    scale = np.exp2(byte - 127.0)
    codes = (blocks / scale).astype(np.float32).astype(dtype).astype(np.float64)
    return np.moveaxis((codes * scale).reshape(v.shape), -1, axis)


WIDE = False


def mx_kscale(k):
    if not WIDE:
        return np.ones(k)
    levels = np.array([10, -10, 5, -5, 0])
    a = np.random.permutation(np.resize(levels, k // 512 * 4)).reshape(k // 512, 4)
    idx = np.arange(k)
    return np.exp2(a[idx // 512, idx % 128 // 32])


BF16 = ml_dtypes.bfloat16


def bf(x):
    return np.asarray(x, np.float32).astype(BF16)


def f64(x):
    return np.asarray(x).astype(np.float64)


B, C_IN, H, W, C_OUT = 4, 512, 64, 64, 128


def _box_sum(x):
    b, h, w, c = x.shape
    xp = np.pad(x, ((0, 0), (1, 1), (1, 1), (0, 0)))
    out = np.zeros_like(x)
    for i in range(3):
        for j in range(3):
            out = out + xp[:, i:i + h, j:j + w, :]
    return out


def setup_inputs():
    s = mx_kscale(C_IN)
    return {"x": bf(np.random.standard_normal((B, C_IN, H, W)) * s[None, :, None, None]),
            "weight": bf(np.random.standard_normal((1, C_IN, C_OUT)) * 3.0 / np.sqrt(C_IN) / s[None, :, None])}


def reference(x, weight):
    x = f64(x)
    weight = f64(weight)
    b, c, h, w = x.shape
    o = weight.shape[-1]
    x1 = np.transpose(x, (0, 2, 3, 1))
    xw = mxq(x1, 3, "e4m3") @ mxq(weight[0], 0, "e4m3")
    deg = _box_sum(np.ones((1, h, w, 1)))
    dinv = 1.0 / np.sqrt(deg)
    y = dinv * _box_sum(dinv * xw)
    return np.transpose(y, (0, 3, 1, 2)).reshape(b, o, w, h)

@@ -1,0 +1,243 @@
+import math
+from contextlib import ExitStack
+
+import concourse.mybir as mybir
+
+F32 = mybir.dt.float32
+BF16 = mybir.dt.bfloat16
+U32 = mybir.dt.uint32
+U8 = mybir.dt.uint8
+I32 = mybir.dt.int32
+FP8X4 = mybir.dt.float8_e4m3fn_x4
+COPY = mybir.ActivationFunctionType.Copy
+ADD = mybir.AluOpType.add
+
+P = 128
+PACK = 4
+B = 4
+C_IN = 512
+SIDE = 64
+C_OUT = 128
+PIX = SIDE * SIDE
+UNIT_ROWS = 8
+UNIT = UNIT_ROWS * SIDE
+UNITS_PER_IMAGE = SIDE // UNIT_ROWS
+N_UNITS = B * UNITS_PER_IMAGE
+CHUNK_ROWS = 16
+CHUNK = CHUNK_ROWS * SIDE
+PADDED = (SIDE + 2) * SIDE
+HALF = SIDE // 2
+PLANE = HALF + 2
+EDGE = math.sqrt(1.5)
+NINTH = 1.0 / 9.0
+V_SHARE_FILL = 336
+FILL_UNITS = 5
+V_SHARE = 176
+
+FLOPS = 2 * B * PIX * C_IN * C_OUT
+
+
+def tile_gcn_layer_t_kernel(tc, x, weight, out):
+    nc = tc.nc
+    with ExitStack() as ctx:
+        keep = ctx.enter_context(tc.tile_pool(name="keep", bufs=1))
+        stage = ctx.enter_context(tc.tile_pool(name="stage", bufs=4))
+        work = ctx.enter_context(tc.tile_pool(name="work", bufs=2))
+        psum = ctx.enter_context(tc.psum_pool(name="psum", bufs=6))
+        xpsum = ctx.enter_context(tc.psum_pool(name="xpsum", bufs=2))
+
+        wraw = keep.tile([P, PACK, C_OUT], BF16, name="wraw")
+        raw = []
+        for b in range(B):
+            rb = keep.tile([P, PACK, PIX], BF16, name="raw%d" % b)
+            raw.append(rb)
+            src = x[b : b + 1].rearrange("b (p t) h w -> p (b t) (h w)", t=PACK)
+            cuts = [0, 8, 16, 32, 64] if b == 0 else [0, 32, 64]
+            for lo, hi in zip(cuts[:-1], cuts[1:]):
+                nc.sync.dma_start(out=rb[:, :, lo * SIDE : hi * SIDE], in_=src[:, :, lo * SIDE : hi * SIDE])
+                if b == 0 and lo == 0:
+                    nc.sync.dma_start(out=wraw[:], in_=weight.rearrange("a (p t) o -> p (a t) o", t=PACK))
+
+        codes = []
+        planes = []
+        for s in range(2):
+            cw = keep.tile([P, PADDED], U32, name="codes%d" % s, align_bytes=64)
+            sc = keep.tile([P, PADDED], U8, name="plane%d" % s, align_bytes=64)
+            for lo in (0, PADDED - SIDE):
+                nc.vector.memset(cw[:, lo : lo + SIDE].bitcast(I32), 0)
+                nc.vector.memset(sc[:, lo : lo + SIDE].bitcast(I32), 0)
+            codes.append(cw)
+            planes.append(sc)
+        rows_t = []
+        for s in range(3):
+            tt = keep.tile([P, CHUNK_ROWS, 2 * PLANE], F32, name="rows%d" % s)
+            nc.vector.memset(tt[:], 0.0)
+            rows_t.append(tt)
+
+        warm = keep.tile([P, 2], F32, name="warm")
+        nc.vector.memset(warm[:, 0:1], 0.0)
+        nc.scalar.activation(out=warm[:, 1:2], in_=warm[:, 0:1], func=COPY, scale=NINTH)
+
+        wgrp = keep.tile([P, C_OUT, PACK], BF16, name="wgrp", align_bytes=64)
+        wcodes = keep.tile([P, C_OUT], U32, name="wcodes", align_bytes=64)
+        wplane = keep.tile([P, C_OUT], U8, name="wplane", align_bytes=64)
+        nc.vector.tensor_copy(out=wgrp[:], in_=wraw[:].rearrange("p t o -> p o t"))
+        nc.vector.quantize_mx(
+            out=wcodes[:].bitcast(FP8X4), scales=wplane[:], in_=wgrp[:].rearrange("p o t -> p (o t)")
+        )
+
+        grouped = {}
+        banks = {}
+        edges = {}
+        edge_sb = {}
+        pairs = {}
+        results = {}
+
+        chunks = []
+        place = {}
+        first = 0
+        while first < N_UNITS:
+            n = 1 if first >= N_UNITS - 2 else 2
+            for i in range(n):
+                place[first + i] = (len(chunks), i * UNIT_ROWS)
+            chunks.append((first, n))
+            first += n
+        ends_at = dict((f + n - 1, c) for c, (f, n) in enumerate(chunks))
+
+        def regroup_views(u, lo, hi):
+            b, g = divmod(u, UNITS_PER_IMAGE)
+            src = raw[b][:, :, g * UNIT + lo : g * UNIT + hi].rearrange("p t (c i) -> p c t i", i=4)
+            dst = grouped[u][:, lo:hi, :].rearrange("p (c i) t -> p c t i", i=4)
+            return dst, src
+
+        def regroup(u):
+            grp = stage.tile([P, UNIT, PACK], BF16, name="grp", tag="grp", align_bytes=64)
+            grouped[u] = grp
+            share = V_SHARE_FILL if u < FILL_UNITS else (0 if u == N_UNITS - 1 else V_SHARE)
+            if share > 0:
+                dst, src = regroup_views(u, 0, share)
+                nc.vector.tensor_copy(out=dst, in_=src)
+            dst, src = regroup_views(u, share, UNIT)
+            nc.scalar.copy(out=dst, in_=src)
+
+        def quantise(u):
+            b, g = divmod(u, UNITS_PER_IMAGE)
+            lo = (1 + g * UNIT_ROWS) * SIDE
+            nc.vector.quantize_mx(
+                out=codes[b % 2][:, lo : lo + UNIT].bitcast(FP8X4),
+                scales=planes[b % 2][:, lo : lo + UNIT],
+                in_=grouped[u][:].rearrange("p w t -> p (w t)"),
+            )
+
+        def mx(acc, b, lo, n, start, stop):
+            nc.tensor.matmul_mx(
+                out=acc,
+                lhsT=wcodes[:].bitcast(FP8X4),
+                lhsT_scale=wplane[:],
+                rhs=codes[b % 2][:, lo : lo + n].bitcast(FP8X4),
+                rhs_scale=planes[b % 2][:, lo : lo + n],
+                start=start,
+                stop=stop,
+            )
+
+        def multiply(u):
+            b, g = divmod(u, UNITS_PER_IMAGE)
+            acc = psum.tile([P, UNIT], F32, name="acc", tag="acc")
+            banks[u] = acc
+            for n, d in enumerate((-1, 0, 1)):
+                mx(acc[:], b, (1 + g * UNIT_ROWS + d) * SIDE, UNIT, n == 0, n == 2)
+            if g == 0 or g == UNITS_PER_IMAGE - 1:
+                xp = xpsum.tile([P, SIDE], F32, name="xp", tag="xp")
+                edges[u] = xp
+                mx(xp[:], b, (1 if g == 0 else SIDE) * SIDE, SIDE, True, True)
+
+        def evacuate(u):
+            g = u % UNITS_PER_IMAGE
+            c, r0 = place[u]
+            tt = rows_t[c % 3]
+            acc = banks[u][:].rearrange("p (r m e) -> p r m e", r=UNIT_ROWS, e=2)
+            nc.scalar.activation(out=tt[:, r0 : r0 + UNIT_ROWS, 2 : 2 + HALF], in_=acc[:, :, :, 1], func=COPY, scale=NINTH)
+            nc.scalar.activation(
+                out=tt[:, r0 : r0 + UNIT_ROWS, PLANE : PLANE + HALF], in_=acc[:, :, :, 0], func=COPY, scale=NINTH
+            )
+            if g == 0 or g == UNITS_PER_IMAGE - 1:
+                xt = work.tile([P, SIDE], F32, name="xt", tag="xt")
+                edge_sb[u] = xt
+                xp = edges[u][:].rearrange("p (m e) -> p m e", e=2)
+                nc.scalar.activation(out=xt[:, 0:HALF], in_=xp[:, :, 1], func=COPY, scale=(EDGE - 1.0) * NINTH)
+                nc.scalar.activation(out=xt[:, HALF:SIDE], in_=xp[:, :, 0], func=COPY, scale=(EDGE - 1.0) * NINTH)
+
+        def weigh(c):
+            f, n = chunks[c]
+            tt = rows_t[c % 3]
+            for u in range(f, f + n):
+                if u in edge_sb:
+                    r0 = place[u][1]
+                    top = u % UNITS_PER_IMAGE == 0
+                    two = r0 if top else r0 + UNIT_ROWS - 2
+                    one = r0 if top else r0 + UNIT_ROWS - 1
+                    near = tt[:, two : two + 2, 2 : 2 + SIDE]
+                    nc.vector.tensor_tensor(
+                        out=near, in0=near, in1=edge_sb[u][:].unsqueeze(1).to_broadcast([P, 2, SIDE]), op=ADD
+                    )
+                    last = tt[:, one : one + 1, 2 : 2 + SIDE]
+                    nc.vector.tensor_scalar_mul(out=last, in0=last, scalar1=EDGE)
+            ends = tt[:, 0 : n * UNIT_ROWS, PLANE - 1 : PLANE + 1]
+            nc.vector.tensor_scalar_mul(out=ends, in0=ends, scalar1=EDGE)
+
+        def pair(c):
+            nr = chunks[c][1] * UNIT_ROWS
+            tt = rows_t[c % 3]
+            q = work.tile([P, CHUNK_ROWS, HALF], F32, name="q", tag="q")
+            pairs[c] = q
+            nc.vector.tensor_tensor(
+                out=q[:, 0:nr, :], in0=tt[:, 0:nr, PLANE : PLANE + HALF], in1=tt[:, 0:nr, 2 : 2 + HALF], op=ADD
+            )
+
+        def third(c):
+            nr = chunks[c][1] * UNIT_ROWS
+            tt = rows_t[c % 3]
+            o = work.tile([P, CHUNK_ROWS, SIDE], F32, name="o", tag="o", bufs=4)
+            results[c] = o
+            outer = (
+                tt[:, 0:nr, :]
+                .rearrange("p r (e l) -> p r e l", e=2)[:, :, :, 1 : 1 + HALF]
+                .rearrange("p r e m -> p r m e")
+            )
+            nc.vector.tensor_tensor(
+                out=o[:, 0:nr, :].rearrange("p r (m e) -> p r m e", e=2),
+                in0=pairs[c][:, 0:nr, :].unsqueeze(3).to_broadcast([P, nr, HALF, 2]),
+                in1=outer,
+                op=ADD,
+            )
+
+        def store(c):
+            f, n = chunks[c]
+            nr = n * UNIT_ROWS
+            b, g = divmod(f, UNITS_PER_IMAGE)
+            o = results[c]
+            sides = o[:, 0:nr, 0 : SIDE : SIDE - 1]
+            nc.vector.tensor_scalar_mul(out=sides, in0=sides, scalar1=EDGE)
+            dst = out[b : b + 1].rearrange("b o h w -> o (b h w)")
+            nc.sync.dma_start(out=dst[:, g * UNIT : g * UNIT + nr * SIDE], in_=o[:, 0:nr, :].rearrange("p r j -> p (r j)"))
+
+        with tc.manual_schedule():
+            for k in range(N_UNITS + 7):
+                a = ends_at.get(k - 5)
+                z = ends_at.get(k - 6)
+                if a is not None:
+                    weigh(a)
+                if z is not None:
+                    third(z)
+                if k < N_UNITS:
+                    regroup(k)
+                if a is not None:
+                    pair(a)
+                if z is not None:
+                    store(z)
+                if 0 <= k - 1 < N_UNITS:
+                    quantise(k - 1)
+                if 0 <= k - 2 < N_UNITS:
+                    multiply(k - 2)
+                if 0 <= k - 3 < N_UNITS:
+                    evacuate(k - 3)

@@ -19,20 +19,29 @@ C_IN = 512
 SIDE = 64
 C_OUT = 128
 PIX = SIDE * SIDE
-UNIT_ROWS = 8
-UNIT = UNIT_ROWS * SIDE
-UNITS_PER_IMAGE = SIDE // UNIT_ROWS
-N_UNITS = B * UNITS_PER_IMAGE
-CHUNK_ROWS = 16
-CHUNK = CHUNK_ROWS * SIDE
+BANK_ROWS = 8
+BANK = BANK_ROWS * SIDE
+BANKS_PER_IMAGE = SIDE // BANK_ROWS
+N_BANKS = B * BANKS_PER_IMAGE
 PADDED = (SIDE + 2) * SIDE
 HALF = SIDE // 2
 PLANE = HALF + 2
 EDGE = math.sqrt(1.5)
 NINTH = 1.0 / 9.0
-V_SHARE_FILL = 336
+
+HALF_ROWS = 32
+RAW_BUFS = 6
+UNIT_ROWS = [8, 8, 8, 8] + [16] * 12 + [8, 8, 8, 8]
+MAX_UNIT = 16 * SIDE
+CHUNK_BANKS = [2, 2] + [4] * 6 + [2, 1, 1]
+MAX_CHUNK_ROWS = 4 * BANK_ROWS
 FILL_UNITS = 5
-V_SHARE = 176
+DRAIN_UNITS = 3
+SHARE_FILL = 0.70
+SHARE = 0.38
+LAG_Q = 1
+LAG_E = 1
+LAG_F = 2
 
 FLOPS = 2 * B * PIX * C_IN * C_OUT
 
@@ -41,23 +50,64 @@ def tile_gcn_layer_t_kernel(tc, x, weight, out):
     nc = tc.nc
     with ExitStack() as ctx:
         keep = ctx.enter_context(tc.tile_pool(name="keep", bufs=1))
-        stage = ctx.enter_context(tc.tile_pool(name="stage", bufs=4))
+        stage = ctx.enter_context(tc.tile_pool(name="stage", bufs=3))
         work = ctx.enter_context(tc.tile_pool(name="work", bufs=2))
         psum = ctx.enter_context(tc.psum_pool(name="psum", bufs=6))
         xpsum = ctx.enter_context(tc.psum_pool(name="xpsum", bufs=2))
+        ctx.enter_context(tc.manual_schedule())
+
+        units = []
+        row = 0
+        for i, n in enumerate(UNIT_ROWS):
+            frac = SHARE_FILL if i < FILL_UNITS else (0.0 if i >= len(UNIT_ROWS) - DRAIN_UNITS else SHARE)
+            units.append((row, n, 8 * int(round(n * SIDE * frac / 8.0))))
+            row += n
+        assert row == B * SIDE
+        unit_of_bank = {}
+        for i, (row0, n, share) in enumerate(units):
+            for bank in range(row0 // BANK_ROWS, (row0 + n) // BANK_ROWS):
+                unit_of_bank[bank] = i
+        chunks = []
+        chunk_of_bank = {}
+        bank = 0
+        for n in CHUNK_BANKS:
+            for i in range(n):
+                chunk_of_bank[bank + i] = len(chunks)
+            chunks.append((bank, n))
+            bank += n
+        assert bank == N_BANKS
+        mm_tick = {}
+        ev_tick = {}
+        for bank in range(N_BANKS):
+            need = unit_of_bank[bank + 1] if bank % BANKS_PER_IMAGE < BANKS_PER_IMAGE - 1 else unit_of_bank[bank]
+            mm_tick[bank] = need + LAG_Q
+            ev_tick[bank] = mm_tick[bank] + LAG_E
+        ch_tick = [ev_tick[f + n - 1] + LAG_F for f, n in chunks]
 
         wraw = keep.tile([P, PACK, C_OUT], BF16, name="wraw")
         raw = []
-        for b in range(B):
-            rb = keep.tile([P, PACK, PIX], BF16, name="raw%d" % b)
+        for s in range(RAW_BUFS):
+            rb = keep.tile([P, PACK, HALF_ROWS * SIDE], BF16, name="raw%d" % s)
             raw.append(rb)
+
+        def load(h):
+            b, part = divmod(h, 2)
             src = x[b : b + 1].rearrange("b (p t) h w -> p (b t) (h w)", t=PACK)
-            cuts = [0, 8, 16, 32, 64] if b == 0 else [0, 32, 64]
+            cuts = [0, 8, 16, 32] if h == 0 else [0, 32]
             for lo, hi in zip(cuts[:-1], cuts[1:]):
-                nc.sync.dma_start(out=rb[:, :, lo * SIDE : hi * SIDE], in_=src[:, :, lo * SIDE : hi * SIDE])
-                if b == 0 and lo == 0:
+                nc.sync.dma_start(
+                    out=raw[h % RAW_BUFS][:, :, lo * SIDE : hi * SIDE],
+                    in_=src[:, :, (part * HALF_ROWS + lo) * SIDE : (part * HALF_ROWS + hi) * SIDE],
+                )
+                if h == 0 and lo == 0:
                     nc.sync.dma_start(out=wraw[:], in_=weight.rearrange("a (p t) o -> p (a t) o", t=PACK))
 
+        for h in range(RAW_BUFS):
+            load(h)
+
+        warm = keep.tile([P, 2], F32, name="warm")
+        nc.vector.memset(warm[:, 0:1], 0.0)
+        nc.scalar.activation(out=warm[:, 1:2], in_=warm[:, 0:1], func=COPY, scale=NINTH)
         codes = []
         planes = []
         for s in range(2):
@@ -70,13 +120,9 @@ def tile_gcn_layer_t_kernel(tc, x, weight, out):
             planes.append(sc)
         rows_t = []
         for s in range(3):
-            tt = keep.tile([P, CHUNK_ROWS, 2 * PLANE], F32, name="rows%d" % s)
+            tt = keep.tile([P, MAX_CHUNK_ROWS, 2 * PLANE], F32, name="rows%d" % s)
             nc.vector.memset(tt[:], 0.0)
             rows_t.append(tt)
-
-        warm = keep.tile([P, 2], F32, name="warm")
-        nc.vector.memset(warm[:, 0:1], 0.0)
-        nc.scalar.activation(out=warm[:, 1:2], in_=warm[:, 0:1], func=COPY, scale=NINTH)
 
         wgrp = keep.tile([P, C_OUT, PACK], BF16, name="wgrp", align_bytes=64)
         wcodes = keep.tile([P, C_OUT], U32, name="wcodes", align_bytes=64)
@@ -93,40 +139,30 @@ def tile_gcn_layer_t_kernel(tc, x, weight, out):
         pairs = {}
         results = {}
 
-        chunks = []
-        place = {}
-        first = 0
-        while first < N_UNITS:
-            n = 1 if first >= N_UNITS - 2 else 2
-            for i in range(n):
-                place[first + i] = (len(chunks), i * UNIT_ROWS)
-            chunks.append((first, n))
-            first += n
-        ends_at = dict((f + n - 1, c) for c, (f, n) in enumerate(chunks))
-
-        def regroup_views(u, lo, hi):
-            b, g = divmod(u, UNITS_PER_IMAGE)
-            src = raw[b][:, :, g * UNIT + lo : g * UNIT + hi].rearrange("p t (c i) -> p c t i", i=4)
-            dst = grouped[u][:, lo:hi, :].rearrange("p (c i) t -> p c t i", i=4)
-            return dst, src
-
         def regroup(u):
-            grp = stage.tile([P, UNIT, PACK], BF16, name="grp", tag="grp", align_bytes=64)
+            row0, n, share = units[u]
+            h, r = divmod(row0, HALF_ROWS)
+            grp = stage.tile([P, MAX_UNIT, PACK], BF16, name="grp", tag="grp", align_bytes=64)
             grouped[u] = grp
-            share = V_SHARE_FILL if u < FILL_UNITS else (0 if u == N_UNITS - 1 else V_SHARE)
-            if share > 0:
-                dst, src = regroup_views(u, 0, share)
-                nc.vector.tensor_copy(out=dst, in_=src)
-            dst, src = regroup_views(u, share, UNIT)
-            nc.scalar.copy(out=dst, in_=src)
+            for lo, hi, on_vector in ((0, share, True), (share, n * SIDE, False)):
+                if hi > lo:
+                    src = raw[h % RAW_BUFS][:, :, r * SIDE + lo : r * SIDE + hi].rearrange("p t (c i) -> p c t i", i=4)
+                    dst = grp[:, lo:hi, :].rearrange("p (c i) t -> p c t i", i=4)
+                    if on_vector:
+                        nc.vector.tensor_copy(out=dst, in_=src)
+                    else:
+                        nc.scalar.copy(out=dst, in_=src)
+            if (row0 + n) % HALF_ROWS == 0 and h + RAW_BUFS < 2 * B:
+                load(h + RAW_BUFS)
 
         def quantise(u):
-            b, g = divmod(u, UNITS_PER_IMAGE)
-            lo = (1 + g * UNIT_ROWS) * SIDE
+            row0, n, share = units[u]
+            b, r = divmod(row0, SIDE)
+            lo = (1 + r) * SIDE
             nc.vector.quantize_mx(
-                out=codes[b % 2][:, lo : lo + UNIT].bitcast(FP8X4),
-                scales=planes[b % 2][:, lo : lo + UNIT],
-                in_=grouped[u][:].rearrange("p w t -> p (w t)"),
+                out=codes[b % 2][:, lo : lo + n * SIDE].bitcast(FP8X4),
+                scales=planes[b % 2][:, lo : lo + n * SIDE],
+                in_=grouped[u][:, 0 : n * SIDE, :].rearrange("p w t -> p (w t)"),
             )
 
         def mx(acc, b, lo, n, start, stop):
@@ -140,64 +176,65 @@ def tile_gcn_layer_t_kernel(tc, x, weight, out):
                 stop=stop,
             )
 
-        def multiply(u):
-            b, g = divmod(u, UNITS_PER_IMAGE)
-            acc = psum.tile([P, UNIT], F32, name="acc", tag="acc")
-            banks[u] = acc
+        def multiply(bank):
+            b, g = divmod(bank, BANKS_PER_IMAGE)
+            acc = psum.tile([P, BANK], F32, name="acc", tag="acc")
+            banks[bank] = acc
             for n, d in enumerate((-1, 0, 1)):
-                mx(acc[:], b, (1 + g * UNIT_ROWS + d) * SIDE, UNIT, n == 0, n == 2)
-            if g == 0 or g == UNITS_PER_IMAGE - 1:
+                mx(acc[:], b, (1 + g * BANK_ROWS + d) * SIDE, BANK, n == 0, n == 2)
+            if g == 0 or g == BANKS_PER_IMAGE - 1:
                 xp = xpsum.tile([P, SIDE], F32, name="xp", tag="xp")
-                edges[u] = xp
+                edges[bank] = xp
                 mx(xp[:], b, (1 if g == 0 else SIDE) * SIDE, SIDE, True, True)
 
-        def evacuate(u):
-            g = u % UNITS_PER_IMAGE
-            c, r0 = place[u]
+        def evacuate(bank):
+            g = bank % BANKS_PER_IMAGE
+            c = chunk_of_bank[bank]
+            r0 = (bank - chunks[c][0]) * BANK_ROWS
             tt = rows_t[c % 3]
-            acc = banks[u][:].rearrange("p (r m e) -> p r m e", r=UNIT_ROWS, e=2)
-            nc.scalar.activation(out=tt[:, r0 : r0 + UNIT_ROWS, 2 : 2 + HALF], in_=acc[:, :, :, 1], func=COPY, scale=NINTH)
+            acc = banks[bank][:].rearrange("p (r m e) -> p r m e", r=BANK_ROWS, e=2)
+            nc.scalar.activation(out=tt[:, r0 : r0 + BANK_ROWS, 2 : 2 + HALF], in_=acc[:, :, :, 1], func=COPY, scale=NINTH)
             nc.scalar.activation(
-                out=tt[:, r0 : r0 + UNIT_ROWS, PLANE : PLANE + HALF], in_=acc[:, :, :, 0], func=COPY, scale=NINTH
+                out=tt[:, r0 : r0 + BANK_ROWS, PLANE : PLANE + HALF], in_=acc[:, :, :, 0], func=COPY, scale=NINTH
             )
-            if g == 0 or g == UNITS_PER_IMAGE - 1:
+            if g == 0 or g == BANKS_PER_IMAGE - 1:
                 xt = work.tile([P, SIDE], F32, name="xt", tag="xt")
-                edge_sb[u] = xt
-                xp = edges[u][:].rearrange("p (m e) -> p m e", e=2)
+                edge_sb[bank] = xt
+                xp = edges[bank][:].rearrange("p (m e) -> p m e", e=2)
                 nc.scalar.activation(out=xt[:, 0:HALF], in_=xp[:, :, 1], func=COPY, scale=(EDGE - 1.0) * NINTH)
                 nc.scalar.activation(out=xt[:, HALF:SIDE], in_=xp[:, :, 0], func=COPY, scale=(EDGE - 1.0) * NINTH)
 
         def weigh(c):
             f, n = chunks[c]
             tt = rows_t[c % 3]
-            for u in range(f, f + n):
-                if u in edge_sb:
-                    r0 = place[u][1]
-                    top = u % UNITS_PER_IMAGE == 0
-                    two = r0 if top else r0 + UNIT_ROWS - 2
-                    one = r0 if top else r0 + UNIT_ROWS - 1
+            for bank in range(f, f + n):
+                if bank in edge_sb:
+                    r0 = (bank - f) * BANK_ROWS
+                    top = bank % BANKS_PER_IMAGE == 0
+                    two = r0 if top else r0 + BANK_ROWS - 2
+                    one = r0 if top else r0 + BANK_ROWS - 1
                     near = tt[:, two : two + 2, 2 : 2 + SIDE]
                     nc.vector.tensor_tensor(
-                        out=near, in0=near, in1=edge_sb[u][:].unsqueeze(1).to_broadcast([P, 2, SIDE]), op=ADD
+                        out=near, in0=near, in1=edge_sb[bank][:].unsqueeze(1).to_broadcast([P, 2, SIDE]), op=ADD
                     )
                     last = tt[:, one : one + 1, 2 : 2 + SIDE]
                     nc.vector.tensor_scalar_mul(out=last, in0=last, scalar1=EDGE)
-            ends = tt[:, 0 : n * UNIT_ROWS, PLANE - 1 : PLANE + 1]
+            ends = tt[:, 0 : n * BANK_ROWS, PLANE - 1 : PLANE + 1]
             nc.vector.tensor_scalar_mul(out=ends, in0=ends, scalar1=EDGE)
 
         def pair(c):
-            nr = chunks[c][1] * UNIT_ROWS
+            nr = chunks[c][1] * BANK_ROWS
             tt = rows_t[c % 3]
-            q = work.tile([P, CHUNK_ROWS, HALF], F32, name="q", tag="q")
+            q = work.tile([P, MAX_CHUNK_ROWS, HALF], F32, name="q", tag="q")
             pairs[c] = q
             nc.vector.tensor_tensor(
                 out=q[:, 0:nr, :], in0=tt[:, 0:nr, PLANE : PLANE + HALF], in1=tt[:, 0:nr, 2 : 2 + HALF], op=ADD
             )
 
         def third(c):
-            nr = chunks[c][1] * UNIT_ROWS
+            nr = chunks[c][1] * BANK_ROWS
             tt = rows_t[c % 3]
-            o = work.tile([P, CHUNK_ROWS, SIDE], F32, name="o", tag="o", bufs=4)
+            o = work.tile([P, MAX_CHUNK_ROWS, SIDE], F32, name="o", tag="o", bufs=3)
             results[c] = o
             outer = (
                 tt[:, 0:nr, :]
@@ -213,31 +250,32 @@ def tile_gcn_layer_t_kernel(tc, x, weight, out):
 
         def store(c):
             f, n = chunks[c]
-            nr = n * UNIT_ROWS
-            b, g = divmod(f, UNITS_PER_IMAGE)
+            nr = n * BANK_ROWS
+            b, g = divmod(f, BANKS_PER_IMAGE)
             o = results[c]
             sides = o[:, 0:nr, 0 : SIDE : SIDE - 1]
             nc.vector.tensor_scalar_mul(out=sides, in0=sides, scalar1=EDGE)
             dst = out[b : b + 1].rearrange("b o h w -> o (b h w)")
-            nc.sync.dma_start(out=dst[:, g * UNIT : g * UNIT + nr * SIDE], in_=o[:, 0:nr, :].rearrange("p r j -> p (r j)"))
+            nc.sync.dma_start(out=dst[:, g * BANK : g * BANK + nr * SIDE], in_=o[:, 0:nr, :].rearrange("p r j -> p (r j)"))
 
-        with tc.manual_schedule():
-            for k in range(N_UNITS + 7):
-                a = ends_at.get(k - 5)
-                z = ends_at.get(k - 6)
-                if a is not None:
-                    weigh(a)
-                if z is not None:
-                    third(z)
-                if k < N_UNITS:
-                    regroup(k)
-                if a is not None:
-                    pair(a)
-                if z is not None:
-                    store(z)
-                if 0 <= k - 1 < N_UNITS:
-                    quantise(k - 1)
-                if 0 <= k - 2 < N_UNITS:
-                    multiply(k - 2)
-                if 0 <= k - 3 < N_UNITS:
-                    evacuate(k - 3)
+        for k in range(max(ch_tick) + 2):
+            first_half = [c for c in range(len(chunks)) if ch_tick[c] == k]
+            second_half = [c for c in range(len(chunks)) if ch_tick[c] + 1 == k]
+            for c in first_half:
+                weigh(c)
+            for c in second_half:
+                third(c)
+            if k < len(units):
+                regroup(k)
+            for c in first_half:
+                pair(c)
+            for c in second_half:
+                store(c)
+            if 0 <= k - LAG_Q < len(units):
+                quantise(k - LAG_Q)
+            for bank in range(N_BANKS):
+                if mm_tick[bank] == k:
+                    multiply(bank)
+            for bank in range(N_BANKS):
+                if ev_tick[bank] == k:
+                    evacuate(bank)

@@ -38,7 +38,7 @@ MAX_CHUNK_ROWS = 4 * BANK_ROWS
 FILL_UNITS = 5
 DRAIN_UNITS = 3
 SHARE_FILL = 0.70
-SHARE = 0.38
+SHARE = 0.32
 LAG_Q = 1
 LAG_E = 1
 LAG_F = 2

@@ -36,9 +36,9 @@ MAX_UNIT = 16 * SIDE
 CHUNK_BANKS = [2, 2] + [4] * 6 + [2, 1, 1]
 MAX_CHUNK_ROWS = 4 * BANK_ROWS
 FILL_UNITS = 5
-DRAIN_UNITS = 3
-SHARE_FILL = 0.70
-SHARE = 0.32
+DRAIN_UNITS = 4
+SHARE_FILL = 0.60
+SHARE = 0.42
 LAG_Q = 1
 LAG_E = 1
 LAG_F = 2
@@ -93,7 +93,7 @@ def tile_gcn_layer_t_kernel(tc, x, weight, out):
         def load(h):
             b, part = divmod(h, 2)
             src = x[b : b + 1].rearrange("b (p t) h w -> p (b t) (h w)", t=PACK)
-            cuts = [0, 8, 16, 32] if h == 0 else [0, 32]
+            cuts = [0, 8, 16, 32] if h == 0 else ([0, 16, 32] if h == 1 else [0, 32])
             for lo, hi in zip(cuts[:-1], cuts[1:]):
                 nc.sync.dma_start(
                     out=raw[h % RAW_BUFS][:, :, lo * SIDE : hi * SIDE],

@@ -2,6 +2,7 @@ import math
 from contextlib import ExitStack
 
 import concourse.mybir as mybir
+from concourse.masks import make_identity
 
 F32 = mybir.dt.float32
 BF16 = mybir.dt.bfloat16
@@ -33,15 +34,23 @@ HALF_ROWS = 32
 RAW_BUFS = 6
 UNIT_ROWS = [8, 8, 8, 8] + [16] * 12 + [8, 8, 8, 8]
 MAX_UNIT = 16 * SIDE
-CHUNK_BANKS = [2, 2] + [4] * 6 + [2, 1, 1]
-MAX_CHUNK_ROWS = 4 * BANK_ROWS
+BAND_BANKS = [[1, 3, 5], [1, 3, 5], [1, 3, 5], [1, 3, 6]]
+VECTOR_CHUNKS = [
+    [[0], [2], [4, 6, 7]],
+    [[0, 2], [4, 6, 7]],
+    [[0, 2], [4, 6, 7]],
+    [[0, 2], [4, 5], [7]],
+]
+MAX_CHUNK_ROWS = 3 * BANK_ROWS
+TILE_PIX = 2 * SIDE
 FILL_UNITS = 5
-DRAIN_UNITS = 4
-SHARE_FILL = 0.60
-SHARE = 0.42
+DRAIN_UNITS = 2
+SHARE_FILL = 0.50
+SHARE = 0.56
 LAG_Q = 1
 LAG_E = 1
 LAG_F = 2
+LAG_B = 1
 
 FLOPS = 2 * B * PIX * C_IN * C_OUT
 
@@ -52,8 +61,9 @@ def tile_gcn_layer_t_kernel(tc, x, weight, out):
         keep = ctx.enter_context(tc.tile_pool(name="keep", bufs=1))
         stage = ctx.enter_context(tc.tile_pool(name="stage", bufs=3))
         work = ctx.enter_context(tc.tile_pool(name="work", bufs=2))
-        psum = ctx.enter_context(tc.psum_pool(name="psum", bufs=6))
-        xpsum = ctx.enter_context(tc.psum_pool(name="xpsum", bufs=2))
+        psum = ctx.enter_context(tc.psum_pool(name="psum", bufs=3))
+        bpsum = ctx.enter_context(tc.psum_pool(name="bpsum", bufs=2))
+        xpsum = ctx.enter_context(tc.psum_pool(name="xpsum", bufs=1))
         ctx.enter_context(tc.manual_schedule())
 
         units = []
@@ -67,22 +77,24 @@ def tile_gcn_layer_t_kernel(tc, x, weight, out):
         for i, (row0, n, share) in enumerate(units):
             for bank in range(row0 // BANK_ROWS, (row0 + n) // BANK_ROWS):
                 unit_of_bank[bank] = i
+        band_banks = set()
         chunks = []
-        chunk_of_bank = {}
-        bank = 0
-        for n in CHUNK_BANKS:
-            for i in range(n):
-                chunk_of_bank[bank + i] = len(chunks)
-            chunks.append((bank, n))
-            bank += n
-        assert bank == N_BANKS
+        place = {}
+        for b in range(B):
+            for g in BAND_BANKS[b]:
+                band_banks.add(b * BANKS_PER_IMAGE + g)
+            for gs in VECTOR_CHUNKS[b]:
+                for i, g in enumerate(gs):
+                    place[b * BANKS_PER_IMAGE + g] = (len(chunks), i * BANK_ROWS)
+                chunks.append([b * BANKS_PER_IMAGE + g for g in gs])
+        assert len(place) + len(band_banks) == N_BANKS
         mm_tick = {}
         ev_tick = {}
         for bank in range(N_BANKS):
             need = unit_of_bank[bank + 1] if bank % BANKS_PER_IMAGE < BANKS_PER_IMAGE - 1 else unit_of_bank[bank]
             mm_tick[bank] = need + LAG_Q
             ev_tick[bank] = mm_tick[bank] + LAG_E
-        ch_tick = [ev_tick[f + n - 1] + LAG_F for f, n in chunks]
+        ch_tick = [max(ev_tick[bank] for bank in banks_c) + LAG_F for banks_c in chunks]
 
         wraw = keep.tile([P, PACK, C_OUT], BF16, name="wraw")
         raw = []
@@ -132,7 +144,20 @@ def tile_gcn_layer_t_kernel(tc, x, weight, out):
             out=wcodes[:].bitcast(FP8X4), scales=wplane[:], in_=wgrp[:].rearrange("p o t -> p (o t)")
         )
 
+        ident = keep.tile([P, P], F32, name="ident")
+        band = keep.tile([P, P], F32, name="band")
+        make_identity(nc, ident[:])
+        iv = ident[:].rearrange("p (a j) -> p a j", a=2)
+        bv = band[:].rearrange("p (a j) -> p a j", a=2)
+        nc.vector.tensor_scalar_mul(out=iv[:, :, 0 : SIDE : SIDE - 1], in0=iv[:, :, 0 : SIDE : SIDE - 1], scalar1=EDGE)
+        nc.vector.tensor_copy(out=band[:], in_=ident[:])
+        nc.vector.tensor_tensor(out=bv[:, :, 1:SIDE], in0=bv[:, :, 1:SIDE], in1=iv[:, :, 0 : SIDE - 1], op=ADD)
+        nc.vector.tensor_tensor(out=bv[:, :, 0 : SIDE - 1], in0=bv[:, :, 0 : SIDE - 1], in1=iv[:, :, 1:SIDE], op=ADD)
+        nc.vector.tensor_scalar_mul(out=band[:], in0=band[:], scalar1=NINTH)
+        nc.vector.tensor_scalar_mul(out=bv[:, :, 0 : SIDE : SIDE - 1], in0=bv[:, :, 0 : SIDE : SIDE - 1], scalar1=EDGE)
+
         grouped = {}
+        summed = {}
         banks = {}
         edges = {}
         edge_sb = {}
@@ -176,6 +201,44 @@ def tile_gcn_layer_t_kernel(tc, x, weight, out):
                 stop=stop,
             )
 
+        def multiply_flipped(bank):
+            b, g = divmod(bank, BANKS_PER_IMAGE)
+            flip = bpsum.tile([P, BANK], F32, name="flip", tag="flip")
+            banks[bank] = flip
+            for t in range(BANK // TILE_PIX):
+                for n, d in enumerate((-1, 0, 1)):
+                    lo = (1 + g * BANK_ROWS + 2 * t + d) * SIDE
+                    nc.tensor.matmul_mx(
+                        out=flip[:, t * C_OUT : (t + 1) * C_OUT],
+                        lhsT=codes[b % 2][:, lo : lo + TILE_PIX].bitcast(FP8X4),
+                        lhsT_scale=planes[b % 2][:, lo : lo + TILE_PIX],
+                        rhs=wcodes[:].bitcast(FP8X4),
+                        rhs_scale=wplane[:],
+                        start=n == 0,
+                        stop=n == 2,
+                    )
+
+        def band_sum(bank):
+            flat = work.tile([P, BANK], F32, name="flat", tag="flat", bufs=2)
+            nc.scalar.copy(out=flat[:], in_=banks[bank][:])
+            wide = bpsum.tile([P, BANK], F32, name="wide", tag="wide")
+            summed[bank] = wide
+            for t in range(BANK // TILE_PIX):
+                nc.tensor.matmul(
+                    out=wide[:, t * TILE_PIX : (t + 1) * TILE_PIX],
+                    lhsT=flat[:, t * C_OUT : (t + 1) * C_OUT],
+                    rhs=band[:],
+                    start=True,
+                    stop=True,
+                )
+
+        def band_store(bank):
+            b, g = divmod(bank, BANKS_PER_IMAGE)
+            ob = work.tile([P, BANK], F32, name="ob", tag="ob", bufs=3)
+            nc.scalar.copy(out=ob[:], in_=summed[bank][:])
+            dst = out[b : b + 1].rearrange("b o h w -> o (b h w)")
+            nc.sync.dma_start(out=dst[:, g * BANK : (g + 1) * BANK], in_=ob[:])
+
         def multiply(bank):
             b, g = divmod(bank, BANKS_PER_IMAGE)
             acc = psum.tile([P, BANK], F32, name="acc", tag="acc")
@@ -189,8 +252,7 @@ def tile_gcn_layer_t_kernel(tc, x, weight, out):
 
         def evacuate(bank):
             g = bank % BANKS_PER_IMAGE
-            c = chunk_of_bank[bank]
-            r0 = (bank - chunks[c][0]) * BANK_ROWS
+            c, r0 = place[bank]
             tt = rows_t[c % 3]
             acc = banks[bank][:].rearrange("p (r m e) -> p r m e", r=BANK_ROWS, e=2)
             nc.scalar.activation(out=tt[:, r0 : r0 + BANK_ROWS, 2 : 2 + HALF], in_=acc[:, :, :, 1], func=COPY, scale=NINTH)
@@ -205,11 +267,11 @@ def tile_gcn_layer_t_kernel(tc, x, weight, out):
                 nc.scalar.activation(out=xt[:, HALF:SIDE], in_=xp[:, :, 0], func=COPY, scale=(EDGE - 1.0) * NINTH)
 
         def weigh(c):
-            f, n = chunks[c]
+            n = len(chunks[c])
             tt = rows_t[c % 3]
-            for bank in range(f, f + n):
+            for bank in chunks[c]:
                 if bank in edge_sb:
-                    r0 = (bank - f) * BANK_ROWS
+                    r0 = place[bank][1]
                     top = bank % BANKS_PER_IMAGE == 0
                     two = r0 if top else r0 + BANK_ROWS - 2
                     one = r0 if top else r0 + BANK_ROWS - 1
@@ -223,7 +285,7 @@ def tile_gcn_layer_t_kernel(tc, x, weight, out):
             nc.vector.tensor_scalar_mul(out=ends, in0=ends, scalar1=EDGE)
 
         def pair(c):
-            nr = chunks[c][1] * BANK_ROWS
+            nr = len(chunks[c]) * BANK_ROWS
             tt = rows_t[c % 3]
             q = work.tile([P, MAX_CHUNK_ROWS, HALF], F32, name="q", tag="q")
             pairs[c] = q
@@ -232,7 +294,7 @@ def tile_gcn_layer_t_kernel(tc, x, weight, out):
             )
 
         def third(c):
-            nr = chunks[c][1] * BANK_ROWS
+            nr = len(chunks[c]) * BANK_ROWS
             tt = rows_t[c % 3]
             o = work.tile([P, MAX_CHUNK_ROWS, SIDE], F32, name="o", tag="o", bufs=3)
             results[c] = o
@@ -249,16 +311,23 @@ def tile_gcn_layer_t_kernel(tc, x, weight, out):
             )
 
         def store(c):
-            f, n = chunks[c]
-            nr = n * BANK_ROWS
-            b, g = divmod(f, BANKS_PER_IMAGE)
+            nr = len(chunks[c]) * BANK_ROWS
+            b = chunks[c][0] // BANKS_PER_IMAGE
             o = results[c]
             sides = o[:, 0:nr, 0 : SIDE : SIDE - 1]
             nc.vector.tensor_scalar_mul(out=sides, in0=sides, scalar1=EDGE)
             dst = out[b : b + 1].rearrange("b o h w -> o (b h w)")
-            nc.sync.dma_start(out=dst[:, g * BANK : g * BANK + nr * SIDE], in_=o[:, 0:nr, :].rearrange("p r j -> p (r j)"))
+            first = 0
+            for i in range(1, len(chunks[c]) + 1):
+                if i == len(chunks[c]) or chunks[c][i] != chunks[c][i - 1] + 1:
+                    g = chunks[c][first] % BANKS_PER_IMAGE
+                    nc.sync.dma_start(
+                        out=dst[:, g * BANK : (g + i - first) * BANK],
+                        in_=o[:, first * BANK_ROWS : i * BANK_ROWS, :].rearrange("p r j -> p (r j)"),
+                    )
+                    first = i
 
-        for k in range(max(ch_tick) + 2):
+        for k in range(max(max(ch_tick) + 2, max(ev_tick[bank] for bank in band_banks) + LAG_B + 1)):
             first_half = [c for c in range(len(chunks)) if ch_tick[c] == k]
             second_half = [c for c in range(len(chunks)) if ch_tick[c] + 1 == k]
             for c in first_half:
@@ -274,8 +343,17 @@ def tile_gcn_layer_t_kernel(tc, x, weight, out):
             if 0 <= k - LAG_Q < len(units):
                 quantise(k - LAG_Q)
             for bank in range(N_BANKS):
-                if mm_tick[bank] == k:
-                    multiply(bank)
+                if bank in band_banks and ev_tick[bank] + LAG_B == k:
+                    band_store(bank)
             for bank in range(N_BANKS):
                 if ev_tick[bank] == k:
-                    evacuate(bank)
+                    if bank in band_banks:
+                        band_sum(bank)
+                    else:
+                        evacuate(bank)
+            for bank in range(N_BANKS):
+                if mm_tick[bank] == k:
+                    if bank in band_banks:
+                        multiply_flipped(bank)
+                    else:
+                        multiply(bank)

@@ -34,23 +34,23 @@ HALF_ROWS = 32
 RAW_BUFS = 6
 UNIT_ROWS = [8, 8, 8, 8] + [16] * 12 + [8, 8, 8, 8]
 MAX_UNIT = 16 * SIDE
-BAND_BANKS = [[1, 3, 5], [1, 3, 5], [1, 3, 5], [1, 3, 6]]
+BAND_BANKS = [[3, 5], [1, 4], [1, 4], [1, 6]]
 VECTOR_CHUNKS = [
-    [[0], [2], [4, 6, 7]],
-    [[0, 2], [4, 6, 7]],
-    [[0, 2], [4, 6, 7]],
-    [[0, 2], [4, 5], [7]],
+    [[0], [1, 2], [4, 6, 7]],
+    [[0, 2, 3], [5, 6, 7]],
+    [[0, 2, 3], [5, 6, 7]],
+    [[0, 2, 3], [4, 5], [7]],
 ]
 MAX_CHUNK_ROWS = 3 * BANK_ROWS
 TILE_PIX = 2 * SIDE
 FILL_UNITS = 5
 DRAIN_UNITS = 2
 SHARE_FILL = 0.50
-SHARE = 0.56
+SHARE = 0.52
 LAG_Q = 1
 LAG_E = 1
 LAG_F = 2
-LAG_B = 1
+LAG_B = 2
 
 FLOPS = 2 * B * PIX * C_IN * C_OUT
 
@@ -158,6 +158,7 @@ def tile_gcn_layer_t_kernel(tc, x, weight, out):
 
         grouped = {}
         summed = {}
+        flats = {}
         banks = {}
         edges = {}
         edge_sb = {}
@@ -218,9 +219,13 @@ def tile_gcn_layer_t_kernel(tc, x, weight, out):
                         stop=n == 2,
                     )
 
-        def band_sum(bank):
+        def band_copy(bank):
             flat = work.tile([P, BANK], F32, name="flat", tag="flat", bufs=2)
+            flats[bank] = flat
             nc.scalar.copy(out=flat[:], in_=banks[bank][:])
+
+        def band_sum(bank):
+            flat = flats[bank]
             wide = bpsum.tile([P, BANK], F32, name="wide", tag="wide")
             summed[bank] = wide
             for t in range(BANK // TILE_PIX):
@@ -348,7 +353,7 @@ def tile_gcn_layer_t_kernel(tc, x, weight, out):
             for bank in range(N_BANKS):
                 if ev_tick[bank] == k:
                     if bank in band_banks:
-                        band_sum(bank)
+                        band_copy(bank)
                     else:
                         evacuate(bank)
             for bank in range(N_BANKS):
@@ -357,3 +362,6 @@ def tile_gcn_layer_t_kernel(tc, x, weight, out):
                         multiply_flipped(bank)
                     else:
                         multiply(bank)
+            for bank in range(N_BANKS):
+                if bank in band_banks and ev_tick[bank] == k:
+                    band_sum(bank)

@@ -64,7 +64,6 @@ def tile_gcn_layer_t_kernel(tc, x, weight, out):
         psum = ctx.enter_context(tc.psum_pool(name="psum", bufs=3))
         bpsum = ctx.enter_context(tc.psum_pool(name="bpsum", bufs=2))
         xpsum = ctx.enter_context(tc.psum_pool(name="xpsum", bufs=1))
-        ctx.enter_context(tc.manual_schedule())
 
         units = []
         row = 0

@@ -12,6 +12,7 @@ I32 = mybir.dt.int32
 FP8X4 = mybir.dt.float8_e4m3fn_x4
 COPY = mybir.ActivationFunctionType.Copy
 ADD = mybir.AluOpType.add
+MULT = mybir.AluOpType.mult
 
 P = 128
 PACK = 4
@@ -34,12 +35,12 @@ HALF_ROWS = 32
 RAW_BUFS = 6
 UNIT_ROWS = [8, 8, 8, 8] + [16] * 12 + [8, 8, 8, 8]
 MAX_UNIT = 16 * SIDE
-BAND_BANKS = [[3, 5], [1, 4], [1, 4], [1, 6]]
+BAND_BANKS = [[0, 7], [0, 7], [0, 7], [0, 7]]
 VECTOR_CHUNKS = [
-    [[0], [1, 2], [4, 6, 7]],
-    [[0, 2, 3], [5, 6, 7]],
-    [[0, 2, 3], [5, 6, 7]],
-    [[0, 2, 3], [4, 5], [7]],
+    [[1], [2, 3], [4, 5, 6]],
+    [[1, 2, 3], [4, 5, 6]],
+    [[1, 2, 3], [4, 5, 6]],
+    [[1, 2, 3], [4, 5], [6]],
 ]
 MAX_CHUNK_ROWS = 3 * BANK_ROWS
 TILE_PIX = 2 * SIDE
@@ -61,9 +62,8 @@ def tile_gcn_layer_t_kernel(tc, x, weight, out):
         keep = ctx.enter_context(tc.tile_pool(name="keep", bufs=1))
         stage = ctx.enter_context(tc.tile_pool(name="stage", bufs=3))
         work = ctx.enter_context(tc.tile_pool(name="work", bufs=2))
-        psum = ctx.enter_context(tc.psum_pool(name="psum", bufs=3))
+        psum = ctx.enter_context(tc.psum_pool(name="psum", bufs=4))
         bpsum = ctx.enter_context(tc.psum_pool(name="bpsum", bufs=2))
-        xpsum = ctx.enter_context(tc.psum_pool(name="xpsum", bufs=1))
 
         units = []
         row = 0
@@ -143,24 +143,40 @@ def tile_gcn_layer_t_kernel(tc, x, weight, out):
             out=wcodes[:].bitcast(FP8X4), scales=wplane[:], in_=wgrp[:].rearrange("p o t -> p (o t)")
         )
 
+        def scaled(dst, src, factor):
+            nc.gpsimd.tensor_scalar(out=dst, in0=src, scalar1=factor, scalar2=0.0, op0=MULT, op1=ADD)
+
         ident = keep.tile([P, P], F32, name="ident")
         band = keep.tile([P, P], F32, name="band")
+        top = keep.tile([P, P], F32, name="top")
+        top2 = keep.tile([P, P], F32, name="top2")
+        bot = keep.tile([P, P], F32, name="bot")
+        bot2 = keep.tile([P, P], F32, name="bot2")
         make_identity(nc, ident[:])
         iv = ident[:].rearrange("p (a j) -> p a j", a=2)
         bv = band[:].rearrange("p (a j) -> p a j", a=2)
-        nc.vector.tensor_scalar_mul(out=iv[:, :, 0 : SIDE : SIDE - 1], in0=iv[:, :, 0 : SIDE : SIDE - 1], scalar1=EDGE)
-        nc.vector.tensor_copy(out=band[:], in_=ident[:])
-        nc.vector.tensor_tensor(out=bv[:, :, 1:SIDE], in0=bv[:, :, 1:SIDE], in1=iv[:, :, 0 : SIDE - 1], op=ADD)
-        nc.vector.tensor_tensor(out=bv[:, :, 0 : SIDE - 1], in0=bv[:, :, 0 : SIDE - 1], in1=iv[:, :, 1:SIDE], op=ADD)
-        nc.vector.tensor_scalar_mul(out=band[:], in0=band[:], scalar1=NINTH)
-        nc.vector.tensor_scalar_mul(out=bv[:, :, 0 : SIDE : SIDE - 1], in0=bv[:, :, 0 : SIDE : SIDE - 1], scalar1=EDGE)
+        scaled(iv[:, :, 0 : SIDE : SIDE - 1], iv[:, :, 0 : SIDE : SIDE - 1], EDGE)
+        scaled(band[:], ident[:], 1.0)
+        nc.gpsimd.tensor_tensor(out=bv[:, :, 1:SIDE], in0=bv[:, :, 1:SIDE], in1=iv[:, :, 0 : SIDE - 1], op=ADD)
+        nc.gpsimd.tensor_tensor(out=bv[:, :, 0 : SIDE - 1], in0=bv[:, :, 0 : SIDE - 1], in1=iv[:, :, 1:SIDE], op=ADD)
+        scaled(band[:], band[:], NINTH)
+        scaled(bv[:, :, 0 : SIDE : SIDE - 1], bv[:, :, 0 : SIDE : SIDE - 1], EDGE)
+        left = band[:, 0:SIDE]
+        right = band[:, SIDE:P]
+        scaled(top[:, 0:SIDE], left, EDGE)
+        scaled(top[:, SIDE:P], right, 1.0)
+        scaled(top2[:, 0:SIDE], left, (EDGE - 1.0) * EDGE)
+        scaled(top2[:, SIDE:P], left, EDGE - 1.0)
+        scaled(bot[:, 0:SIDE], left, 1.0)
+        scaled(bot[:, SIDE:P], right, EDGE)
+        scaled(bot2[:, 0:SIDE], right, EDGE - 1.0)
+        scaled(bot2[:, SIDE:P], right, (EDGE - 1.0) * EDGE)
 
         grouped = {}
         summed = {}
         flats = {}
         banks = {}
-        edges = {}
-        edge_sb = {}
+        extras = {}
         pairs = {}
         results = {}
 
@@ -217,24 +233,40 @@ def tile_gcn_layer_t_kernel(tc, x, weight, out):
                         start=n == 0,
                         stop=n == 2,
                     )
+            lone = bpsum.tile([P, BANK], F32, name="lone", tag="flip")
+            extras[bank] = lone
+            lo = (1 if g == 0 else SIDE - 1) * SIDE
+            nc.tensor.matmul_mx(
+                out=lone[:, 0:C_OUT],
+                lhsT=codes[b % 2][:, lo : lo + TILE_PIX].bitcast(FP8X4),
+                lhsT_scale=planes[b % 2][:, lo : lo + TILE_PIX],
+                rhs=wcodes[:].bitcast(FP8X4),
+                rhs_scale=wplane[:],
+                start=True,
+                stop=True,
+            )
 
         def band_copy(bank):
             flat = work.tile([P, BANK], F32, name="flat", tag="flat", bufs=2)
-            flats[bank] = flat
+            flat2 = work.tile([P, C_OUT], F32, name="flat2", tag="flat2", bufs=2)
+            flats[bank] = (flat, flat2)
             nc.scalar.copy(out=flat[:], in_=banks[bank][:])
+            nc.scalar.copy(out=flat2[:], in_=extras[bank][:, 0:C_OUT])
 
         def band_sum(bank):
-            flat = flats[bank]
+            g = bank % BANKS_PER_IMAGE
+            flat, flat2 = flats[bank]
             wide = bpsum.tile([P, BANK], F32, name="wide", tag="wide")
             summed[bank] = wide
-            for t in range(BANK // TILE_PIX):
-                nc.tensor.matmul(
-                    out=wide[:, t * TILE_PIX : (t + 1) * TILE_PIX],
-                    lhsT=flat[:, t * C_OUT : (t + 1) * C_OUT],
-                    rhs=band[:],
-                    start=True,
-                    stop=True,
-                )
+            last = BANK // TILE_PIX - 1
+            for t in range(last + 1):
+                dst = wide[:, t * TILE_PIX : (t + 1) * TILE_PIX]
+                mine = flat[:, t * C_OUT : (t + 1) * C_OUT]
+                if (g == 0 and t == 0) or (g != 0 and t == last):
+                    nc.tensor.matmul(out=dst, lhsT=mine, rhs=(top if g == 0 else bot)[:], start=True, stop=False)
+                    nc.tensor.matmul(out=dst, lhsT=flat2[:], rhs=(top2 if g == 0 else bot2)[:], start=False, stop=True)
+                else:
+                    nc.tensor.matmul(out=dst, lhsT=mine, rhs=band[:], start=True, stop=True)
 
         def band_store(bank):
             b, g = divmod(bank, BANKS_PER_IMAGE)
@@ -249,42 +281,20 @@ def tile_gcn_layer_t_kernel(tc, x, weight, out):
             banks[bank] = acc
             for n, d in enumerate((-1, 0, 1)):
                 mx(acc[:], b, (1 + g * BANK_ROWS + d) * SIDE, BANK, n == 0, n == 2)
-            if g == 0 or g == BANKS_PER_IMAGE - 1:
-                xp = xpsum.tile([P, SIDE], F32, name="xp", tag="xp")
-                edges[bank] = xp
-                mx(xp[:], b, (1 if g == 0 else SIDE) * SIDE, SIDE, True, True)
 
         def evacuate(bank):
-            g = bank % BANKS_PER_IMAGE
             c, r0 = place[bank]
             tt = rows_t[c % 3]
-            acc = banks[bank][:].rearrange("p (r m e) -> p r m e", r=BANK_ROWS, e=2)
-            nc.scalar.activation(out=tt[:, r0 : r0 + BANK_ROWS, 2 : 2 + HALF], in_=acc[:, :, :, 1], func=COPY, scale=NINTH)
             nc.scalar.activation(
-                out=tt[:, r0 : r0 + BANK_ROWS, PLANE : PLANE + HALF], in_=acc[:, :, :, 0], func=COPY, scale=NINTH
+                out=tt[:, r0 : r0 + BANK_ROWS, 2 : 2 + SIDE].rearrange("p r (e m) -> p r e m", e=2),
+                in_=banks[bank][:].rearrange("p (r m e) -> p r e m", r=BANK_ROWS, e=2)[:, :, ::-1, :],
+                func=COPY,
+                scale=NINTH,
             )
-            if g == 0 or g == BANKS_PER_IMAGE - 1:
-                xt = work.tile([P, SIDE], F32, name="xt", tag="xt")
-                edge_sb[bank] = xt
-                xp = edges[bank][:].rearrange("p (m e) -> p m e", e=2)
-                nc.scalar.activation(out=xt[:, 0:HALF], in_=xp[:, :, 1], func=COPY, scale=(EDGE - 1.0) * NINTH)
-                nc.scalar.activation(out=xt[:, HALF:SIDE], in_=xp[:, :, 0], func=COPY, scale=(EDGE - 1.0) * NINTH)
 
         def weigh(c):
             n = len(chunks[c])
             tt = rows_t[c % 3]
-            for bank in chunks[c]:
-                if bank in edge_sb:
-                    r0 = place[bank][1]
-                    top = bank % BANKS_PER_IMAGE == 0
-                    two = r0 if top else r0 + BANK_ROWS - 2
-                    one = r0 if top else r0 + BANK_ROWS - 1
-                    near = tt[:, two : two + 2, 2 : 2 + SIDE]
-                    nc.vector.tensor_tensor(
-                        out=near, in0=near, in1=edge_sb[bank][:].unsqueeze(1).to_broadcast([P, 2, SIDE]), op=ADD
-                    )
-                    last = tt[:, one : one + 1, 2 : 2 + SIDE]
-                    nc.vector.tensor_scalar_mul(out=last, in0=last, scalar1=EDGE)
             ends = tt[:, 0 : n * BANK_ROWS, PLANE - 1 : PLANE + 1]
             nc.vector.tensor_scalar_mul(out=ends, in0=ends, scalar1=EDGE)
 

@@ -12,7 +12,6 @@ I32 = mybir.dt.int32
 FP8X4 = mybir.dt.float8_e4m3fn_x4
 COPY = mybir.ActivationFunctionType.Copy
 ADD = mybir.AluOpType.add
-MULT = mybir.AluOpType.mult
 
 P = 128
 PACK = 4
@@ -132,7 +131,8 @@ def tile_gcn_layer_t_kernel(tc, x, weight, out):
         rows_t = []
         for s in range(3):
             tt = keep.tile([P, MAX_CHUNK_ROWS, 2 * PLANE], F32, name="rows%d" % s)
-            nc.vector.memset(tt[:], 0.0)
+            nc.vector.memset(tt[:, :, 0:2], 0.0)
+            nc.vector.memset(tt[:, :, 2 * PLANE - 2 : 2 * PLANE], 0.0)
             rows_t.append(tt)
 
         wgrp = keep.tile([P, C_OUT, PACK], BF16, name="wgrp", align_bytes=64)
@@ -144,7 +144,7 @@ def tile_gcn_layer_t_kernel(tc, x, weight, out):
         )
 
         def scaled(dst, src, factor):
-            nc.gpsimd.tensor_scalar(out=dst, in0=src, scalar1=factor, scalar2=0.0, op0=MULT, op1=ADD)
+            nc.vector.tensor_scalar_mul(out=dst, in0=src, scalar1=factor)
 
         ident = keep.tile([P, P], F32, name="ident")
         band = keep.tile([P, P], F32, name="band")
@@ -157,8 +157,8 @@ def tile_gcn_layer_t_kernel(tc, x, weight, out):
         bv = band[:].rearrange("p (a j) -> p a j", a=2)
         scaled(iv[:, :, 0 : SIDE : SIDE - 1], iv[:, :, 0 : SIDE : SIDE - 1], EDGE)
         scaled(band[:], ident[:], 1.0)
-        nc.gpsimd.tensor_tensor(out=bv[:, :, 1:SIDE], in0=bv[:, :, 1:SIDE], in1=iv[:, :, 0 : SIDE - 1], op=ADD)
-        nc.gpsimd.tensor_tensor(out=bv[:, :, 0 : SIDE - 1], in0=bv[:, :, 0 : SIDE - 1], in1=iv[:, :, 1:SIDE], op=ADD)
+        nc.vector.tensor_tensor(out=bv[:, :, 1:SIDE], in0=bv[:, :, 1:SIDE], in1=iv[:, :, 0 : SIDE - 1], op=ADD)
+        nc.vector.tensor_tensor(out=bv[:, :, 0 : SIDE - 1], in0=bv[:, :, 0 : SIDE - 1], in1=iv[:, :, 1:SIDE], op=ADD)
         scaled(band[:], band[:], NINTH)
         scaled(bv[:, :, 0 : SIDE : SIDE - 1], bv[:, :, 0 : SIDE : SIDE - 1], EDGE)
         left = band[:, 0:SIDE]

@@ -68,7 +68,7 @@ def tile_gcn_layer_t_kernel(tc, x, weight, out):
         row = 0
         for i, n in enumerate(UNIT_ROWS):
             frac = SHARE_FILL if i < FILL_UNITS else (0.0 if i >= len(UNIT_ROWS) - DRAIN_UNITS else SHARE)
-            units.append((row, n, 8 * int(round(n * SIDE * frac / 8.0))))
+            units.append((row, n, 16 * int(round(n * SIDE * frac / 16.0))))
             row += n
         assert row == B * SIDE
         unit_of_bank = {}
@@ -187,8 +187,8 @@ def tile_gcn_layer_t_kernel(tc, x, weight, out):
             grouped[u] = grp
             for lo, hi, on_vector in ((0, share, True), (share, n * SIDE, False)):
                 if hi > lo:
-                    src = raw[h % RAW_BUFS][:, :, r * SIDE + lo : r * SIDE + hi].rearrange("p t (c i) -> p c t i", i=4)
-                    dst = grp[:, lo:hi, :].rearrange("p (c i) t -> p c t i", i=4)
+                    src = raw[h % RAW_BUFS][:, :, r * SIDE + lo : r * SIDE + hi].rearrange("p t (c i) -> p c t i", i=8)
+                    dst = grp[:, lo:hi, :].rearrange("p (c i) t -> p c t i", i=8)
                     if on_vector:
                         nc.vector.tensor_copy(out=dst, in_=src)
                     else:

@@ -32,7 +32,7 @@ NINTH = 1.0 / 9.0
 
 HALF_ROWS = 32
 RAW_BUFS = 6
-UNIT_ROWS = [8, 8, 8, 8] + [16] * 12 + [8, 8, 8, 8]
+UNIT_ROWS = [4, 4, 8, 8, 8] + [16] * 12 + [8, 8, 8, 8]
 MAX_UNIT = 16 * SIDE
 BAND_BANKS = [[0, 7], [0, 7], [0, 7], [0, 7]]
 VECTOR_CHUNKS = [
@@ -43,8 +43,8 @@ VECTOR_CHUNKS = [
 ]
 MAX_CHUNK_ROWS = 3 * BANK_ROWS
 TILE_PIX = 2 * SIDE
-FILL_UNITS = 5
-DRAIN_UNITS = 2
+FILL_UNITS = 6
+DRAIN_UNITS = 1
 SHARE_FILL = 0.50
 SHARE = 0.52
 LAG_Q = 1
@@ -59,7 +59,7 @@ def tile_gcn_layer_t_kernel(tc, x, weight, out):
     nc = tc.nc
     with ExitStack() as ctx:
         keep = ctx.enter_context(tc.tile_pool(name="keep", bufs=1))
-        stage = ctx.enter_context(tc.tile_pool(name="stage", bufs=3))
+        stage = ctx.enter_context(tc.tile_pool(name="stage", bufs=4))
         work = ctx.enter_context(tc.tile_pool(name="work", bufs=2))
         psum = ctx.enter_context(tc.psum_pool(name="psum", bufs=4))
         bpsum = ctx.enter_context(tc.psum_pool(name="bpsum", bufs=2))
@@ -103,7 +103,7 @@ def tile_gcn_layer_t_kernel(tc, x, weight, out):
         def load(h):
             b, part = divmod(h, 2)
             src = x[b : b + 1].rearrange("b (p t) h w -> p (b t) (h w)", t=PACK)
-            cuts = [0, 8, 16, 32] if h == 0 else ([0, 16, 32] if h == 1 else [0, 32])
+            cuts = [0, 4, 8, 16, 32] if h == 0 else ([0, 16, 32] if h == 1 else [0, 32])
             for lo, hi in zip(cuts[:-1], cuts[1:]):
                 nc.sync.dma_start(
                     out=raw[h % RAW_BUFS][:, :, lo * SIDE : hi * SIDE],
@@ -247,8 +247,8 @@ def tile_gcn_layer_t_kernel(tc, x, weight, out):
             )
 
         def band_copy(bank):
-            flat = work.tile([P, BANK], F32, name="flat", tag="flat", bufs=2)
-            flat2 = work.tile([P, C_OUT], F32, name="flat2", tag="flat2", bufs=2)
+            flat = work.tile([P, BANK], F32, name="flat", tag="flat", bufs=3)
+            flat2 = work.tile([P, C_OUT], F32, name="flat2", tag="flat2", bufs=3)
             flats[bank] = (flat, flat2)
             nc.scalar.copy(out=flat[:], in_=banks[bank][:])
             nc.scalar.copy(out=flat2[:], in_=extras[bank][:, 0:C_OUT])
@@ -301,7 +301,7 @@ def tile_gcn_layer_t_kernel(tc, x, weight, out):
         def pair(c):
             nr = len(chunks[c]) * BANK_ROWS
             tt = rows_t[c % 3]
-            q = work.tile([P, MAX_CHUNK_ROWS, HALF], F32, name="q", tag="q")
+            q = work.tile([P, MAX_CHUNK_ROWS, HALF], F32, name="q", tag="q", bufs=3)
             pairs[c] = q
             nc.vector.tensor_tensor(
                 out=q[:, 0:nr, :], in0=tt[:, 0:nr, PLANE : PLANE + HALF], in1=tt[:, 0:nr, 2 : 2 + HALF], op=ADD

@@ -34,11 +34,11 @@ HALF_ROWS = 32
 RAW_BUFS = 6
 UNIT_ROWS = [4, 4, 8, 8, 8] + [16] * 12 + [8, 8, 8, 8]
 MAX_UNIT = 16 * SIDE
-BAND_BANKS = [[0, 7], [0, 7], [0, 7], [0, 7]]
+BAND_BANKS = [[0, 7], [0, 4, 7], [0, 4, 7], [0, 7]]
 VECTOR_CHUNKS = [
     [[1], [2, 3], [4, 5, 6]],
-    [[1, 2, 3], [4, 5, 6]],
-    [[1, 2, 3], [4, 5, 6]],
+    [[1, 2, 3], [5, 6]],
+    [[1, 2, 3], [5, 6]],
     [[1, 2, 3], [4, 5], [6]],
 ]
 MAX_CHUNK_ROWS = 3 * BANK_ROWS
@@ -46,7 +46,7 @@ TILE_PIX = 2 * SIDE
 FILL_UNITS = 6
 DRAIN_UNITS = 1
 SHARE_FILL = 0.50
-SHARE = 0.52
+SHARE = 0.545
 LAG_Q = 1
 LAG_E = 1
 LAG_F = 2
@@ -233,38 +233,41 @@ def tile_gcn_layer_t_kernel(tc, x, weight, out):
                         start=n == 0,
                         stop=n == 2,
                     )
-            lone = bpsum.tile([P, BANK], F32, name="lone", tag="flip")
-            extras[bank] = lone
-            lo = (1 if g == 0 else SIDE - 1) * SIDE
-            nc.tensor.matmul_mx(
-                out=lone[:, 0:C_OUT],
-                lhsT=codes[b % 2][:, lo : lo + TILE_PIX].bitcast(FP8X4),
-                lhsT_scale=planes[b % 2][:, lo : lo + TILE_PIX],
-                rhs=wcodes[:].bitcast(FP8X4),
-                rhs_scale=wplane[:],
-                start=True,
-                stop=True,
-            )
+            if g == 0 or g == BANKS_PER_IMAGE - 1:
+                lone = bpsum.tile([P, BANK], F32, name="lone", tag="flip")
+                extras[bank] = lone
+                lo = (1 if g == 0 else SIDE - 1) * SIDE
+                nc.tensor.matmul_mx(
+                    out=lone[:, 0:C_OUT],
+                    lhsT=codes[b % 2][:, lo : lo + TILE_PIX].bitcast(FP8X4),
+                    lhsT_scale=planes[b % 2][:, lo : lo + TILE_PIX],
+                    rhs=wcodes[:].bitcast(FP8X4),
+                    rhs_scale=wplane[:],
+                    start=True,
+                    stop=True,
+                )
 
         def band_copy(bank):
             flat = work.tile([P, BANK], F32, name="flat", tag="flat", bufs=3)
-            flat2 = work.tile([P, C_OUT], F32, name="flat2", tag="flat2", bufs=3)
-            flats[bank] = (flat, flat2)
             nc.scalar.copy(out=flat[:], in_=banks[bank][:])
-            nc.scalar.copy(out=flat2[:], in_=extras[bank][:, 0:C_OUT])
+            flats[bank] = [flat]
+            if bank in extras:
+                flat2 = work.tile([P, C_OUT], F32, name="flat2", tag="flat2", bufs=3)
+                nc.scalar.copy(out=flat2[:], in_=extras[bank][:, 0:C_OUT])
+                flats[bank].append(flat2)
 
         def band_sum(bank):
             g = bank % BANKS_PER_IMAGE
-            flat, flat2 = flats[bank]
+            flat = flats[bank][0]
             wide = bpsum.tile([P, BANK], F32, name="wide", tag="wide")
             summed[bank] = wide
             last = BANK // TILE_PIX - 1
             for t in range(last + 1):
                 dst = wide[:, t * TILE_PIX : (t + 1) * TILE_PIX]
                 mine = flat[:, t * C_OUT : (t + 1) * C_OUT]
-                if (g == 0 and t == 0) or (g != 0 and t == last):
+                if (g == 0 and t == 0) or (g == BANKS_PER_IMAGE - 1 and t == last):
                     nc.tensor.matmul(out=dst, lhsT=mine, rhs=(top if g == 0 else bot)[:], start=True, stop=False)
-                    nc.tensor.matmul(out=dst, lhsT=flat2[:], rhs=(top2 if g == 0 else bot2)[:], start=False, stop=True)
+                    nc.tensor.matmul(out=dst, lhsT=flats[bank][1][:], rhs=(top2 if g == 0 else bot2)[:], start=False, stop=True)
                 else:
                     nc.tensor.matmul(out=dst, lhsT=mine, rhs=band[:], start=True, stop=True)
 

@@ -44,7 +44,7 @@ VECTOR_CHUNKS = [
 MAX_CHUNK_ROWS = 3 * BANK_ROWS
 TILE_PIX = 2 * SIDE
 FILL_UNITS = 6
-DRAIN_UNITS = 1
+DRAIN_UNITS = 0
 SHARE_FILL = 0.50
 SHARE = 0.545
 LAG_Q = 1

import math
from contextlib import ExitStack

import concourse.mybir as mybir
from concourse.masks import make_identity

F32 = mybir.dt.float32
BF16 = mybir.dt.bfloat16
U32 = mybir.dt.uint32
U8 = mybir.dt.uint8
I32 = mybir.dt.int32
FP8X4 = mybir.dt.float8_e4m3fn_x4
COPY = mybir.ActivationFunctionType.Copy
ADD = mybir.AluOpType.add

P = 128
PACK = 4
B = 4
C_IN = 512
SIDE = 64
C_OUT = 128
PIX = SIDE * SIDE
BANK_ROWS = 8
BANK = BANK_ROWS * SIDE
BANKS_PER_IMAGE = SIDE // BANK_ROWS
N_BANKS = B * BANKS_PER_IMAGE
PADDED = (SIDE + 2) * SIDE
HALF = SIDE // 2
PLANE = HALF + 2
EDGE = math.sqrt(1.5)
NINTH = 1.0 / 9.0

HALF_ROWS = 32
RAW_BUFS = 6
UNIT_ROWS = [4, 4, 8, 8, 8] + [16] * 12 + [8, 8, 8, 8]
MAX_UNIT = 16 * SIDE
BAND_BANKS = [[0, 7], [0, 4, 7], [0, 4, 7], [0, 7]]
VECTOR_CHUNKS = [
    [[1], [2, 3], [4, 5, 6]],
    [[1, 2, 3], [5, 6]],
    [[1, 2, 3], [5, 6]],
    [[1, 2, 3], [4, 5], [6]],
]
MAX_CHUNK_ROWS = 3 * BANK_ROWS
TILE_PIX = 2 * SIDE
FILL_UNITS = 6
DRAIN_UNITS = 0
SHARE_FILL = 0.50
SHARE = 0.545
LAG_Q = 1
LAG_E = 1
LAG_F = 2
LAG_B = 2

FLOPS = 2 * B * PIX * C_IN * C_OUT


def tile_gcn_layer_t_kernel(tc, x, weight, out):
    nc = tc.nc
    with ExitStack() as ctx:
        keep = ctx.enter_context(tc.tile_pool(name="keep", bufs=1))
        stage = ctx.enter_context(tc.tile_pool(name="stage", bufs=4))
        work = ctx.enter_context(tc.tile_pool(name="work", bufs=2))
        psum = ctx.enter_context(tc.psum_pool(name="psum", bufs=4))
        bpsum = ctx.enter_context(tc.psum_pool(name="bpsum", bufs=2))

        units = []
        row = 0
        for i, n in enumerate(UNIT_ROWS):
            frac = SHARE_FILL if i < FILL_UNITS else (0.0 if i >= len(UNIT_ROWS) - DRAIN_UNITS else SHARE)
            units.append((row, n, 16 * int(round(n * SIDE * frac / 16.0))))
            row += n
        assert row == B * SIDE
        unit_of_bank = {}
        for i, (row0, n, share) in enumerate(units):
            for bank in range(row0 // BANK_ROWS, (row0 + n) // BANK_ROWS):
                unit_of_bank[bank] = i
        band_banks = set()
        chunks = []
        place = {}
        for b in range(B):
            for g in BAND_BANKS[b]:
                band_banks.add(b * BANKS_PER_IMAGE + g)
            for gs in VECTOR_CHUNKS[b]:
                for i, g in enumerate(gs):
                    place[b * BANKS_PER_IMAGE + g] = (len(chunks), i * BANK_ROWS)
                chunks.append([b * BANKS_PER_IMAGE + g for g in gs])
        assert len(place) + len(band_banks) == N_BANKS
        mm_tick = {}
        ev_tick = {}
        for bank in range(N_BANKS):
            need = unit_of_bank[bank + 1] if bank % BANKS_PER_IMAGE < BANKS_PER_IMAGE - 1 else unit_of_bank[bank]
            mm_tick[bank] = need + LAG_Q
            ev_tick[bank] = mm_tick[bank] + LAG_E
        ch_tick = [max(ev_tick[bank] for bank in banks_c) + LAG_F for banks_c in chunks]

        wraw = keep.tile([P, PACK, C_OUT], BF16, name="wraw")
        raw = []
        for s in range(RAW_BUFS):
            rb = keep.tile([P, PACK, HALF_ROWS * SIDE], BF16, name="raw%d" % s)
            raw.append(rb)

        def load(h):
            b, part = divmod(h, 2)
            src = x[b : b + 1].rearrange("b (p t) h w -> p (b t) (h w)", t=PACK)
            cuts = [0, 4, 8, 16, 32] if h == 0 else ([0, 16, 32] if h == 1 else [0, 32])
            for lo, hi in zip(cuts[:-1], cuts[1:]):
                nc.sync.dma_start(
                    out=raw[h % RAW_BUFS][:, :, lo * SIDE : hi * SIDE],
                    in_=src[:, :, (part * HALF_ROWS + lo) * SIDE : (part * HALF_ROWS + hi) * SIDE],
                )
                if h == 0 and lo == 0:
                    nc.sync.dma_start(out=wraw[:], in_=weight.rearrange("a (p t) o -> p (a t) o", t=PACK))

        for h in range(RAW_BUFS):
            load(h)

        warm = keep.tile([P, 2], F32, name="warm")
        nc.vector.memset(warm[:, 0:1], 0.0)
        nc.scalar.activation(out=warm[:, 1:2], in_=warm[:, 0:1], func=COPY, scale=NINTH)
        codes = []
        planes = []
        for s in range(2):
            cw = keep.tile([P, PADDED], U32, name="codes%d" % s, align_bytes=64)
            sc = keep.tile([P, PADDED], U8, name="plane%d" % s, align_bytes=64)
            for lo in (0, PADDED - SIDE):
                nc.vector.memset(cw[:, lo : lo + SIDE].bitcast(I32), 0)
                nc.vector.memset(sc[:, lo : lo + SIDE].bitcast(I32), 0)
            codes.append(cw)
            planes.append(sc)
        rows_t = []
        for s in range(3):
            tt = keep.tile([P, MAX_CHUNK_ROWS, 2 * PLANE], F32, name="rows%d" % s)
            nc.vector.memset(tt[:, :, 0:2], 0.0)
            nc.vector.memset(tt[:, :, 2 * PLANE - 2 : 2 * PLANE], 0.0)
            rows_t.append(tt)

        wgrp = keep.tile([P, C_OUT, PACK], BF16, name="wgrp", align_bytes=64)
        wcodes = keep.tile([P, C_OUT], U32, name="wcodes", align_bytes=64)
        wplane = keep.tile([P, C_OUT], U8, name="wplane", align_bytes=64)
        nc.vector.tensor_copy(out=wgrp[:], in_=wraw[:].rearrange("p t o -> p o t"))
        nc.vector.quantize_mx(
            out=wcodes[:].bitcast(FP8X4), scales=wplane[:], in_=wgrp[:].rearrange("p o t -> p (o t)")
        )

        def scaled(dst, src, factor):
            nc.vector.tensor_scalar_mul(out=dst, in0=src, scalar1=factor)

        ident = keep.tile([P, P], F32, name="ident")
        band = keep.tile([P, P], F32, name="band")
        top = keep.tile([P, P], F32, name="top")
        top2 = keep.tile([P, P], F32, name="top2")
        bot = keep.tile([P, P], F32, name="bot")
        bot2 = keep.tile([P, P], F32, name="bot2")
        make_identity(nc, ident[:])
        iv = ident[:].rearrange("p (a j) -> p a j", a=2)
        bv = band[:].rearrange("p (a j) -> p a j", a=2)
        scaled(iv[:, :, 0 : SIDE : SIDE - 1], iv[:, :, 0 : SIDE : SIDE - 1], EDGE)
        scaled(band[:], ident[:], 1.0)
        nc.vector.tensor_tensor(out=bv[:, :, 1:SIDE], in0=bv[:, :, 1:SIDE], in1=iv[:, :, 0 : SIDE - 1], op=ADD)
        nc.vector.tensor_tensor(out=bv[:, :, 0 : SIDE - 1], in0=bv[:, :, 0 : SIDE - 1], in1=iv[:, :, 1:SIDE], op=ADD)
        scaled(band[:], band[:], NINTH)
        scaled(bv[:, :, 0 : SIDE : SIDE - 1], bv[:, :, 0 : SIDE : SIDE - 1], EDGE)
        left = band[:, 0:SIDE]
        right = band[:, SIDE:P]
        scaled(top[:, 0:SIDE], left, EDGE)
        scaled(top[:, SIDE:P], right, 1.0)
        scaled(top2[:, 0:SIDE], left, (EDGE - 1.0) * EDGE)
        scaled(top2[:, SIDE:P], left, EDGE - 1.0)
        scaled(bot[:, 0:SIDE], left, 1.0)
        scaled(bot[:, SIDE:P], right, EDGE)
        scaled(bot2[:, 0:SIDE], right, EDGE - 1.0)
        scaled(bot2[:, SIDE:P], right, (EDGE - 1.0) * EDGE)

        grouped = {}
        summed = {}
        flats = {}
        banks = {}
        extras = {}
        pairs = {}
        results = {}

        def regroup(u):
            row0, n, share = units[u]
            h, r = divmod(row0, HALF_ROWS)
            grp = stage.tile([P, MAX_UNIT, PACK], BF16, name="grp", tag="grp", align_bytes=64)
            grouped[u] = grp
            for lo, hi, on_vector in ((0, share, True), (share, n * SIDE, False)):
                if hi > lo:
                    src = raw[h % RAW_BUFS][:, :, r * SIDE + lo : r * SIDE + hi].rearrange("p t (c i) -> p c t i", i=8)
                    dst = grp[:, lo:hi, :].rearrange("p (c i) t -> p c t i", i=8)
                    if on_vector:
                        nc.vector.tensor_copy(out=dst, in_=src)
                    else:
                        nc.scalar.copy(out=dst, in_=src)
            if (row0 + n) % HALF_ROWS == 0 and h + RAW_BUFS < 2 * B:
                load(h + RAW_BUFS)

        def quantise(u):
            row0, n, share = units[u]
            b, r = divmod(row0, SIDE)
            lo = (1 + r) * SIDE
            nc.vector.quantize_mx(
                out=codes[b % 2][:, lo : lo + n * SIDE].bitcast(FP8X4),
                scales=planes[b % 2][:, lo : lo + n * SIDE],
                in_=grouped[u][:, 0 : n * SIDE, :].rearrange("p w t -> p (w t)"),
            )

        def mx(acc, b, lo, n, start, stop):
            nc.tensor.matmul_mx(
                out=acc,
                lhsT=wcodes[:].bitcast(FP8X4),
                lhsT_scale=wplane[:],
                rhs=codes[b % 2][:, lo : lo + n].bitcast(FP8X4),
                rhs_scale=planes[b % 2][:, lo : lo + n],
                start=start,
                stop=stop,
            )

        def multiply_flipped(bank):
            b, g = divmod(bank, BANKS_PER_IMAGE)
            flip = bpsum.tile([P, BANK], F32, name="flip", tag="flip")
            banks[bank] = flip
            for t in range(BANK // TILE_PIX):
                for n, d in enumerate((-1, 0, 1)):
                    lo = (1 + g * BANK_ROWS + 2 * t + d) * SIDE
                    nc.tensor.matmul_mx(
                        out=flip[:, t * C_OUT : (t + 1) * C_OUT],
                        lhsT=codes[b % 2][:, lo : lo + TILE_PIX].bitcast(FP8X4),
                        lhsT_scale=planes[b % 2][:, lo : lo + TILE_PIX],
                        rhs=wcodes[:].bitcast(FP8X4),
                        rhs_scale=wplane[:],
                        start=n == 0,
                        stop=n == 2,
                    )
            if g == 0 or g == BANKS_PER_IMAGE - 1:
                lone = bpsum.tile([P, BANK], F32, name="lone", tag="flip")
                extras[bank] = lone
                lo = (1 if g == 0 else SIDE - 1) * SIDE
                nc.tensor.matmul_mx(
                    out=lone[:, 0:C_OUT],
                    lhsT=codes[b % 2][:, lo : lo + TILE_PIX].bitcast(FP8X4),
                    lhsT_scale=planes[b % 2][:, lo : lo + TILE_PIX],
                    rhs=wcodes[:].bitcast(FP8X4),
                    rhs_scale=wplane[:],
                    start=True,
                    stop=True,
                )

        def band_copy(bank):
            flat = work.tile([P, BANK], F32, name="flat", tag="flat", bufs=3)
            nc.scalar.copy(out=flat[:], in_=banks[bank][:])
            flats[bank] = [flat]
            if bank in extras:
                flat2 = work.tile([P, C_OUT], F32, name="flat2", tag="flat2", bufs=3)
                nc.scalar.copy(out=flat2[:], in_=extras[bank][:, 0:C_OUT])
                flats[bank].append(flat2)

        def band_sum(bank):
            g = bank % BANKS_PER_IMAGE
            flat = flats[bank][0]
            wide = bpsum.tile([P, BANK], F32, name="wide", tag="wide")
            summed[bank] = wide
            last = BANK // TILE_PIX - 1
            for t in range(last + 1):
                dst = wide[:, t * TILE_PIX : (t + 1) * TILE_PIX]
                mine = flat[:, t * C_OUT : (t + 1) * C_OUT]
                if (g == 0 and t == 0) or (g == BANKS_PER_IMAGE - 1 and t == last):
                    nc.tensor.matmul(out=dst, lhsT=mine, rhs=(top if g == 0 else bot)[:], start=True, stop=False)
                    nc.tensor.matmul(out=dst, lhsT=flats[bank][1][:], rhs=(top2 if g == 0 else bot2)[:], start=False, stop=True)
                else:
                    nc.tensor.matmul(out=dst, lhsT=mine, rhs=band[:], start=True, stop=True)

        def band_store(bank):
            b, g = divmod(bank, BANKS_PER_IMAGE)
            ob = work.tile([P, BANK], F32, name="ob", tag="ob", bufs=3)
            nc.scalar.copy(out=ob[:], in_=summed[bank][:])
            dst = out[b : b + 1].rearrange("b o h w -> o (b h w)")
            nc.sync.dma_start(out=dst[:, g * BANK : (g + 1) * BANK], in_=ob[:])

        def multiply(bank):
            b, g = divmod(bank, BANKS_PER_IMAGE)
            acc = psum.tile([P, BANK], F32, name="acc", tag="acc")
            banks[bank] = acc
            for n, d in enumerate((-1, 0, 1)):
                mx(acc[:], b, (1 + g * BANK_ROWS + d) * SIDE, BANK, n == 0, n == 2)

        def evacuate(bank):
            c, r0 = place[bank]
            tt = rows_t[c % 3]
            nc.scalar.activation(
                out=tt[:, r0 : r0 + BANK_ROWS, 2 : 2 + SIDE].rearrange("p r (e m) -> p r e m", e=2),
                in_=banks[bank][:].rearrange("p (r m e) -> p r e m", r=BANK_ROWS, e=2)[:, :, ::-1, :],
                func=COPY,
                scale=NINTH,
            )

        def weigh(c):
            n = len(chunks[c])
            tt = rows_t[c % 3]
            ends = tt[:, 0 : n * BANK_ROWS, PLANE - 1 : PLANE + 1]
            nc.vector.tensor_scalar_mul(out=ends, in0=ends, scalar1=EDGE)

        def pair(c):
            nr = len(chunks[c]) * BANK_ROWS
            tt = rows_t[c % 3]
            q = work.tile([P, MAX_CHUNK_ROWS, HALF], F32, name="q", tag="q", bufs=3)
            pairs[c] = q
            nc.vector.tensor_tensor(
                out=q[:, 0:nr, :], in0=tt[:, 0:nr, PLANE : PLANE + HALF], in1=tt[:, 0:nr, 2 : 2 + HALF], op=ADD
            )

        def third(c):
            nr = len(chunks[c]) * BANK_ROWS
            tt = rows_t[c % 3]
            o = work.tile([P, MAX_CHUNK_ROWS, SIDE], F32, name="o", tag="o", bufs=3)
            results[c] = o
            outer = (
                tt[:, 0:nr, :]
                .rearrange("p r (e l) -> p r e l", e=2)[:, :, :, 1 : 1 + HALF]
                .rearrange("p r e m -> p r m e")
            )
            nc.vector.tensor_tensor(
                out=o[:, 0:nr, :].rearrange("p r (m e) -> p r m e", e=2),
                in0=pairs[c][:, 0:nr, :].unsqueeze(3).to_broadcast([P, nr, HALF, 2]),
                in1=outer,
                op=ADD,
            )

        def store(c):
            nr = len(chunks[c]) * BANK_ROWS
            b = chunks[c][0] // BANKS_PER_IMAGE
            o = results[c]
            sides = o[:, 0:nr, 0 : SIDE : SIDE - 1]
            nc.vector.tensor_scalar_mul(out=sides, in0=sides, scalar1=EDGE)
            dst = out[b : b + 1].rearrange("b o h w -> o (b h w)")
            first = 0
            for i in range(1, len(chunks[c]) + 1):
                if i == len(chunks[c]) or chunks[c][i] != chunks[c][i - 1] + 1:
                    g = chunks[c][first] % BANKS_PER_IMAGE
                    nc.sync.dma_start(
                        out=dst[:, g * BANK : (g + i - first) * BANK],
                        in_=o[:, first * BANK_ROWS : i * BANK_ROWS, :].rearrange("p r j -> p (r j)"),
                    )
                    first = i

        for k in range(max(max(ch_tick) + 2, max(ev_tick[bank] for bank in band_banks) + LAG_B + 1)):
            first_half = [c for c in range(len(chunks)) if ch_tick[c] == k]
            second_half = [c for c in range(len(chunks)) if ch_tick[c] + 1 == k]
            for c in first_half:
                weigh(c)
            for c in second_half:
                third(c)
            if k < len(units):
                regroup(k)
            for c in first_half:
                pair(c)
            for c in second_half:
                store(c)
            if 0 <= k - LAG_Q < len(units):
                quantise(k - LAG_Q)
            for bank in range(N_BANKS):
                if bank in band_banks and ev_tick[bank] + LAG_B == k:
                    band_store(bank)
            for bank in range(N_BANKS):
                if ev_tick[bank] == k:
                    if bank in band_banks:
                        band_copy(bank)
                    else:
                        evacuate(bank)
            for bank in range(N_BANKS):
                if mm_tick[bank] == k:
                    if bank in band_banks:
                        multiply_flipped(bank)
                    else:
                        multiply(bank)
            for bank in range(N_BANKS):
                if bank in band_banks and ev_tick[bank] == k:
                    band_sum(bank)
